import numpy as np
import ml_dtypes


def mxq(x, axis, fmt="e4m3"):
    dtype, down = {"e4m3": (ml_dtypes.float8_e4m3fn, 7), "e5m2": (ml_dtypes.float8_e5m2, 14)}[fmt]
    v = np.moveaxis(np.asarray(x, np.float32).astype(ml_dtypes.bfloat16).astype(np.float64), axis, -1)
    blocks = v.reshape(v.shape[:-1] + (-1, 32))
    amax = np.abs(blocks).max(-1, keepdims=True)
    byte = np.maximum(np.where(amax > 0, np.frexp(amax)[1] - 1 + 127, 0) - down, 1)
    scale = np.exp2(byte - 127.0)
    codes = (blocks / scale).astype(np.float32).astype(dtype).astype(np.float64)
    return np.moveaxis((codes * scale).reshape(v.shape), -1, axis)


WIDE = False


def mx_kscale(k):
    if not WIDE:
        return np.ones(k)
    levels = np.array([10, -10, 5, -5, 0])
    if k % 512:
        return np.exp2(np.random.permutation(np.resize(levels, k // 32))).repeat(32)
    a = np.empty((k // 512, 16))
    for p in range(k // 512):
        a[p, :8] = np.random.permutation(np.resize(levels, 8))
        for g in range(8):
            far = levels[np.abs(levels - a[p, g]) >= 10]
            a[p, g + 8] = far[np.random.randint(len(far))]
    return np.exp2(a.ravel()).repeat(32)


BF16 = ml_dtypes.bfloat16


def bf(x):
    return np.asarray(x, np.float32).astype(BF16)


def f64(x):
    return np.asarray(x).astype(np.float64)


B, N, G, C_IN, C_OUT, D = 4, 512, 255, 2, 2, 256
F = (G + 1) * C_IN


def laplacian_with_self_loop(adj):
    m = adj + np.eye(adj.shape[0])
    d = m.sum(1) ** -0.5
    return (m * d[None, :]).T * d[None, :]


def setup_inputs():
    s = mx_kscale(N)
    t = mx_kscale(F)
    a = 0.25 * np.sqrt(N)
    lap = laplacian_with_self_loop(np.random.random_sample((N, N)))
    return {"x": bf(np.random.standard_normal((B, N, C_IN)) * a / s[None, :, None] * t[None, None, :C_IN]),
            "h": bf(np.random.standard_normal((B, N, G * C_IN)) * a / s[None, :, None] * t[None, None, C_IN:]),
            "laplacian": bf(lap * s[None, :]),
            "weights": bf(np.random.standard_normal((G + 1, D, C_IN, C_OUT)) * 3.0 / np.sqrt(F) / t.reshape(G + 1, C_IN)[:, None, :, None]),
            "biases": bf(np.random.standard_normal((D, C_OUT)) * 0.1)}


def reference(x, h, laplacian, weights, biases):
    xh = np.concatenate([f64(x)[:, :, None, :], f64(h).reshape(B, N, G, C_IN)], axis=2)
    ax = mxq(f64(laplacian), 1, "e4m3") @ mxq(xh.reshape(B, N, F), 1, "e4m3")
    w = f64(weights).transpose(0, 2, 1, 3).reshape(F, D * C_OUT)
    out = (mxq(ax, 2, "e4m3") @ mxq(w, 0, "e4m3")) + f64(biases).reshape(D * C_OUT)
    return out.reshape(B, N * D, C_OUT)

@@ -1,0 +1,229 @@
+from contextlib import ExitStack
+
+import concourse.mybir as mybir
+from concourse.masks import make_identity
+
+F32 = mybir.dt.float32
+BF16 = mybir.dt.bfloat16
+U32 = mybir.dt.uint32
+U8 = mybir.dt.uint8
+FP8X4 = mybir.dt.float8_e4m3fn_x4
+ADD = mybir.AluOpType.add
+
+P = 128
+PACK = 4
+B = 4
+NODES = 512
+CH = 2
+GS = 256
+FEAT = GS * CH
+OUTS = 512
+NODE_TILES = NODES // P
+HALF = GS // 2
+LOWER = 0
+UPPER = 1
+LATE = 2
+FLOPS = 2 * 2 * B * NODES * FEAT * OUTS
+
+
+def tile_tgcngraphconvolution_pa_kernel(tc, x, h, laplacian, weights, biases, out):
+    nc = tc.nc
+    with ExitStack() as ctx:
+        keep = ctx.enter_context(tc.tile_pool(name="keep", bufs=1))
+        first_banks = ctx.enter_context(tc.psum_pool(name="first_banks", bufs=4))
+        second_banks = ctx.enter_context(tc.psum_pool(name="second_banks", bufs=4))
+        ctx.enter_context(tc.manual_schedule())
+
+        bias_row = keep.tile([P, OUTS], BF16)
+        nc.vector.memset(bias_row[:], 0.0)
+        ones = keep.tile([P, P], BF16)
+        nc.vector.memset(ones[:], 1.0)
+        identity = keep.tile([P, P], F32)
+        make_identity(nc, identity[:])
+
+        lap_sb = keep.tile([P, NODE_TILES * NODES], BF16)
+        x_sb = keep.tile([P, B, PACK * CH], BF16)
+        w_sb = keep.tile([P, 2, OUTS * CH], BF16)
+        h_sb = [keep.tile([P, PACK * (FEAT - CH)], BF16, name="h_sb%d" % b) for b in range(B)]
+        with nc.allow_non_contiguous_dma(reason="x has only two values a node"):
+            nc.scalar.dma_start(out=x_sb[:], in_=x.rearrange("b (q t) c -> q b (t c)", t=PACK))
+        nc.scalar.dma_start(out=bias_row[0:1, :], in_=biases.rearrange("(a d) o -> a (d o)", a=1))
+
+        def load_h(b):
+            nc.sync.dma_start(out=h_sb[b][:], in_=h[b].rearrange("(q t) f -> q (t f)", t=PACK))
+
+        load_h(0)
+        nc.sync.dma_start(out=lap_sb[:], in_=laplacian.rearrange("(p i) n -> p (i n)", i=NODE_TILES))
+        load_h(1)
+        nc.sync.dma_start(out=w_sb[:], in_=weights.rearrange("(p u) d c o -> p u (d c o)", u=2))
+        load_h(2)
+        load_h(3)
+
+        bias_sb = keep.tile([P, OUTS], F32)
+        lap_grouped = keep.tile([P, NODES * PACK], BF16, align_bytes=64)
+        lap_codes = keep.tile([P, NODES], U32, align_bytes=64)
+        lap_scales = keep.tile([P, NODES], U8, align_bytes=64)
+        w_grouped = keep.tile([P, OUTS, PACK], BF16, align_bytes=64)
+        w_codes = keep.tile([P, OUTS], U32, align_bytes=64)
+        w_scales = keep.tile([P, OUTS], U8, align_bytes=64)
+        xh_grouped = []
+        xh_codes = []
+        xh_scales = []
+        ax_grouped = []
+        ax_codes = []
+        ax_scales = []
+        out_sb = []
+        for b in range(B):
+            xh_grouped.append(keep.tile([P, 2, CH, HALF, PACK], BF16, name="xh_grouped%d" % b, align_bytes=64))
+            xh_codes.append(keep.tile([P, FEAT], U32, name="xh_codes%d" % b, align_bytes=64))
+            xh_scales.append(keep.tile([P, FEAT], U8, name="xh_scales%d" % b, align_bytes=64))
+            ax_grouped.append(keep.tile([P, NODE_TILES, P, PACK], BF16, name="ax_grouped%d" % b, align_bytes=64))
+            ax_codes.append(keep.tile([P, NODES], U32, name="ax_codes%d" % b, align_bytes=64))
+            ax_scales.append(keep.tile([P, NODES], U8, name="ax_scales%d" % b, align_bytes=64))
+            out_sb.append(keep.tile([P, NODE_TILES, OUTS], F32, name="out_sb%d" % b))
+        out_rows = out.rearrange("b (p i d) o -> b p i (d o)", i=NODE_TILES, d=OUTS // 2)
+        products = {}
+
+        def h_by_unit(b):
+            return h_sb[b][:].rearrange("q (t g c) -> q g t c", t=PACK, c=CH)
+
+        def regroup_lower(b):
+            nc.scalar.copy(out=xh_grouped[b][:, LOWER, :, 1:HALF, :].rearrange("q c g t -> q g t c"),
+                           in_=h_by_unit(b)[:, 1:GS - 2:2])
+            nc.scalar.copy(out=xh_grouped[b][:, LOWER, :, 0, :].rearrange("q c t -> q t c"),
+                           in_=x_sb[:, b].rearrange("q (t c) -> q t c", c=CH))
+
+        def regroup_upper(b):
+            nc.vector.tensor_copy(out=xh_grouped[b][:, UPPER].rearrange("q c g t -> q g t c"),
+                                  in_=h_by_unit(b)[:, 0:GS - 1:2])
+
+        def quantise_xh(b, half):
+            cols = slice(half * CH * HALF, (half + 1) * CH * HALF)
+            nc.vector.quantize_mx(out=xh_codes[b][:, cols].bitcast(FP8X4), scales=xh_scales[b][:, cols],
+                                  in_=xh_grouped[b][:, half].rearrange("q c g t -> q (c g t)"))
+
+        lap_words = lap_sb[:].bitcast(F32)
+        lap_grouped_words = lap_grouped[:].bitcast(F32).rearrange("q (m u) -> q m u", u=2)
+
+        def transpose_laplacian(pair):
+            bank = first_banks.tile([P, 2, 2, P], F32, tag="first", name="lap_t%d" % pair)
+            for i in range(2):
+                for u in range(2):
+                    start = (2 * pair + i) * 2 * P
+                    nc.tensor.transpose(bank[:, i, u, :], lap_words[:, start + u:start + 2 * P:2], identity[:])
+            nc.scalar.copy(
+                out=lap_grouped_words[:, 2 * P * pair:2 * P * (pair + 1), :].rearrange("q (i m) u -> q i m u", i=2),
+                in_=bank[:].rearrange("q i u m -> q i m u"))
+
+        def quantise_laplacian(pair):
+            cols = slice(2 * P * pair, 2 * P * (pair + 1))
+            nc.vector.quantize_mx(out=lap_codes[:, cols].bitcast(FP8X4), scales=lap_scales[:, cols],
+                                  in_=lap_grouped[:, 2 * P * PACK * pair:2 * P * PACK * (pair + 1)])
+
+        def regroup_weights(part):
+            nc.vector.tensor_copy(
+                out=w_grouped[:, part * OUTS // 2:(part + 1) * OUTS // 2, :].rearrange(
+                    "p (d o) (u c) -> p d u c o", o=2, c=CH),
+                in_=w_sb[:, :, part * OUTS:(part + 1) * OUTS].rearrange("p u (d c o) -> p d u c o", c=CH, o=2))
+
+        def quantise_weights():
+            nc.vector.quantize_mx(out=w_codes[:].bitcast(FP8X4), scales=w_scales[:],
+                                  in_=w_grouped[:].rearrange("p n t -> p (n t)"))
+
+        def spread_bias():
+            bank = second_banks.tile([P, OUTS], F32, tag="second", name="bias_bank")
+            nc.tensor.matmul(out=bank[:], lhsT=ones[:], rhs=bias_row[:], start=True, stop=True)
+            nc.scalar.copy(out=bias_sb[:], in_=bank[:])
+
+        def first_matmul(b):
+            for i in range(NODE_TILES):
+                bank = first_banks.tile([P, PACK, P], F32, tag="first", name="ax_bank%d_%d" % (b, i))
+                for j in range(PACK):
+                    nc.tensor.matmul_mx(
+                        out=bank[:, j, :],
+                        lhsT=xh_codes[b][:, j * P:(j + 1) * P].bitcast(FP8X4),
+                        lhsT_scale=xh_scales[b][:, j * P:(j + 1) * P],
+                        rhs=lap_codes[:, i * P:(i + 1) * P].bitcast(FP8X4),
+                        rhs_scale=lap_scales[:, i * P:(i + 1) * P],
+                        start=True, stop=True)
+                nc.scalar.copy(out=ax_grouped[b][:, i], in_=bank[:].rearrange("p j m -> p m j"))
+
+        def quantise_ax(b, node_tiles):
+            cols = slice(node_tiles[0] * P, (node_tiles[-1] + 1) * P)
+            nc.vector.quantize_mx(
+                out=ax_codes[b][:, cols].bitcast(FP8X4), scales=ax_scales[b][:, cols],
+                in_=ax_grouped[b][:, node_tiles[0]:node_tiles[-1] + 1].rearrange("p i m j -> p (i m j)"))
+
+        def second_matmul(b, node_tiles):
+            for i in node_tiles:
+                bank = second_banks.tile([P, OUTS], F32, tag="second", name="out_bank%d_%d" % (b, i))
+                products[(b, i)] = bank
+                nc.tensor.matmul_mx(
+                    out=bank[:],
+                    lhsT=ax_codes[b][:, i * P:(i + 1) * P].bitcast(FP8X4),
+                    lhsT_scale=ax_scales[b][:, i * P:(i + 1) * P],
+                    rhs=w_codes[:].bitcast(FP8X4),
+                    rhs_scale=w_scales[:],
+                    start=True, stop=True)
+
+        def add_bias(b, i):
+            nc.vector.tensor_tensor(out=out_sb[b][:, i, :], in0=products[(b, i)][:], in1=bias_sb[:], op=ADD)
+
+        def store(b, node_tiles):
+            nc.sync.dma_start(out=out_rows[b][:, node_tiles[0]:node_tiles[-1] + 1, :],
+                              in_=out_sb[b][:, node_tiles[0]:node_tiles[-1] + 1, :])
+
+        def launch(b):
+            quantise_xh(b, LOWER)
+            if b + 1 < B:
+                regroup_lower(b + 1)
+            first_matmul(b)
+
+        regroup_upper(0)
+        regroup_lower(0)
+        quantise_xh(0, UPPER)
+        quantise_xh(0, LOWER)
+        transpose_laplacian(0)
+        transpose_laplacian(1)
+        regroup_upper(1)
+        quantise_laplacian(0)
+        quantise_laplacian(1)
+        regroup_lower(1)
+        quantise_xh(1, UPPER)
+        regroup_weights(0)
+        quantise_xh(1, LOWER)
+        regroup_weights(1)
+        first_matmul(0)
+        spread_bias()
+        regroup_lower(LATE)
+        first_matmul(1)
+
+        groups = [(b, pair) for b in range(B) for pair in ((0, 1), (2, 3))]
+        last = len(groups) - 1
+        for k in range(last + 2):
+            if k <= last:
+                b, pair = groups[k]
+                ahead = b + 2
+                if ahead < B and pair[0] == 0:
+                    regroup_upper(ahead)
+                if k < last:
+                    quantise_ax(b, pair)
+                if k == last - 1:
+                    quantise_ax(*groups[last])
+                if k == 0:
+                    quantise_weights()
+                second_matmul(b, pair)
+                if ahead < B and pair[0] != 0:
+                    quantise_xh(ahead, UPPER)
+                    if ahead != LATE:
+                        launch(ahead)
+            if k > 0:
+                b, pair = groups[k - 1]
+                for i in pair:
+                    add_bias(b, i)
+                    if k - 1 == last:
+                        store(b, (i,))
+                if k - 1 < last:
+                    store(b, pair)
+                if k - 1 == 0:
+                    launch(LATE)

@@ -81,6 +81,7 @@ def tile_tgcngraphconvolution_pa_kernel(tc, x, h, laplacian, weights, biases, ou
             ax_codes.append(keep.tile([P, NODES], U32, name="ax_codes%d" % b, align_bytes=64))
             ax_scales.append(keep.tile([P, NODES], U8, name="ax_scales%d" % b, align_bytes=64))
             out_sb.append(keep.tile([P, NODE_TILES, OUTS], F32, name="out_sb%d" % b))
+        plain_sb = [keep.tile([P, OUTS], F32, name="plain_sb%d" % j) for j in range(2)]
         out_rows = out.rearrange("b (p i d) o -> b p i (d o)", i=NODE_TILES, d=OUTS // 2)
         products = {}
 
@@ -169,6 +170,14 @@ def tile_tgcngraphconvolution_pa_kernel(tc, x, h, laplacian, weights, biases, ou
         def add_bias(b, i):
             nc.vector.tensor_tensor(out=out_sb[b][:, i, :], in0=products[(b, i)][:], in1=bias_sb[:], op=ADD)
 
+        def add_bias_beside(b, node_tiles):
+            for i in node_tiles:
+                nc.scalar.copy(out=plain_sb[i % 2][:], in_=products[(b, i)][:])
+            for i in node_tiles:
+                nc.gpsimd.tensor_tensor(out=out_sb[b][:, i, :], in0=plain_sb[i % 2][:], in1=bias_sb[:], op=ADD)
+            for i in node_tiles:
+                nc.scalar.dma_start(out=out_rows[b][:, i:i + 1, :], in_=out_sb[b][:, i:i + 1, :])
+
         def store(b, node_tiles):
             nc.sync.dma_start(out=out_rows[b][:, node_tiles[0]:node_tiles[-1] + 1, :],
                               in_=out_sb[b][:, node_tiles[0]:node_tiles[-1] + 1, :])
@@ -217,13 +226,15 @@ def tile_tgcngraphconvolution_pa_kernel(tc, x, h, laplacian, weights, biases, ou
                     quantise_xh(ahead, UPPER)
                     if ahead != LATE:
                         launch(ahead)
-            if k > 0:
+            if k - 1 == last - 2:
+                add_bias_beside(*groups[k - 1])
+            elif k > 0:
                 b, pair = groups[k - 1]
                 for i in pair:
                     add_bias(b, i)
-                    if k - 1 == last:
+                    if k - 1 >= last - 1:
                         store(b, (i,))
-                if k - 1 < last:
+                if k - 1 < last - 1:
                     store(b, pair)
                 if k - 1 == 0:
                     launch(LATE)

@@ -41,7 +41,7 @@ def tile_tgcngraphconvolution_pa_kernel(tc, x, h, laplacian, weights, biases, ou
         identity = keep.tile([P, P], F32)
         make_identity(nc, identity[:])
 
-        lap_sb = keep.tile([P, NODE_TILES * NODES], BF16)
+        lap_sb = [keep.tile([P, 2 * NODES], BF16, name="lap_sb%d" % pair) for pair in range(2)]
         x_sb = keep.tile([P, B, PACK * CH], BF16)
         w_sb = keep.tile([P, 2, OUTS * CH], BF16)
         h_sb = [keep.tile([P, PACK * (FEAT - CH)], BF16, name="h_sb%d" % b) for b in range(B)]
@@ -53,7 +53,9 @@ def tile_tgcngraphconvolution_pa_kernel(tc, x, h, laplacian, weights, biases, ou
             nc.sync.dma_start(out=h_sb[b][:], in_=h[b].rearrange("(q t) f -> q (t f)", t=PACK))
 
         load_h(0)
-        nc.sync.dma_start(out=lap_sb[:], in_=laplacian.rearrange("(p i) n -> p (i n)", i=NODE_TILES))
+        for pair in range(2):
+            nc.sync.dma_start(out=lap_sb[pair][:].rearrange("p (i n) -> p i n", i=2),
+                              in_=laplacian.rearrange("(p i) n -> p i n", i=NODE_TILES)[:, 2 * pair:2 * pair + 2, :])
         load_h(1)
         nc.sync.dma_start(out=w_sb[:], in_=weights.rearrange("(p u) d c o -> p u (d c o)", u=2))
         load_h(2)
@@ -103,15 +105,15 @@ def tile_tgcngraphconvolution_pa_kernel(tc, x, h, laplacian, weights, biases, ou
             nc.vector.quantize_mx(out=xh_codes[b][:, cols].bitcast(FP8X4), scales=xh_scales[b][:, cols],
                                   in_=xh_grouped[b][:, half].rearrange("q c g t -> q (c g t)"))
 
-        lap_words = lap_sb[:].bitcast(F32)
+        lap_words = [lap_sb[pair][:].bitcast(F32) for pair in range(2)]
         lap_grouped_words = lap_grouped[:].bitcast(F32).rearrange("q (m u) -> q m u", u=2)
 
         def transpose_laplacian(pair):
             bank = first_banks.tile([P, 2, 2, P], F32, tag="first", name="lap_t%d" % pair)
             for i in range(2):
                 for u in range(2):
-                    start = (2 * pair + i) * 2 * P
-                    nc.tensor.transpose(bank[:, i, u, :], lap_words[:, start + u:start + 2 * P:2], identity[:])
+                    start = i * 2 * P
+                    nc.tensor.transpose(bank[:, i, u, :], lap_words[pair][:, start + u:start + 2 * P:2], identity[:])
             nc.scalar.copy(
                 out=lap_grouped_words[:, 2 * P * pair:2 * P * (pair + 1), :].rearrange("q (i m) u -> q i m u", i=2),
                 in_=bank[:].rearrange("q i u m -> q i m u"))
@@ -194,8 +196,8 @@ def tile_tgcngraphconvolution_pa_kernel(tc, x, h, laplacian, weights, biases, ou
         quantise_xh(0, LOWER)
         transpose_laplacian(0)
         transpose_laplacian(1)
-        regroup_upper(1)
         quantise_laplacian(0)
+        regroup_upper(1)
         quantise_laplacian(1)
         regroup_lower(1)
         quantise_xh(1, UPPER)

@@ -23,6 +23,7 @@ HALF = GS // 2
 LOWER = 0
 UPPER = 1
 LATE = 2
+WARM_UP = 16
 FLOPS = 2 * 2 * B * NODES * FEAT * OUTS
 
 
@@ -34,10 +35,10 @@ def tile_tgcngraphconvolution_pa_kernel(tc, x, h, laplacian, weights, biases, ou
         second_banks = ctx.enter_context(tc.psum_pool(name="second_banks", bufs=4))
         ctx.enter_context(tc.manual_schedule())
 
-        bias_row = keep.tile([P, OUTS], BF16)
-        nc.vector.memset(bias_row[:], 0.0)
         ones = keep.tile([P, P], BF16)
         nc.vector.memset(ones[:], 1.0)
+        bias_row = keep.tile([P, OUTS], BF16)
+        nc.vector.memset(bias_row[:], 0.0)
         identity = keep.tile([P, P], F32)
         make_identity(nc, identity[:])
 
@@ -190,6 +191,9 @@ def tile_tgcngraphconvolution_pa_kernel(tc, x, h, laplacian, weights, biases, ou
                 regroup_lower(b + 1)
             first_matmul(b)
 
+        warm_bank = first_banks.tile([P, P], F32, tag="first", name="warm_bank")
+        for w in range(WARM_UP):
+            nc.tensor.matmul(out=warm_bank[:], lhsT=ones[:], rhs=ones[:], start=True, stop=True)
         regroup_upper(0)
         regroup_lower(0)
         quantise_xh(0, UPPER)

@@ -9,6 +9,7 @@ U32 = mybir.dt.uint32
 U8 = mybir.dt.uint8
 FP8X4 = mybir.dt.float8_e4m3fn_x4
 ADD = mybir.AluOpType.add
+MULT = mybir.AluOpType.mult
 
 P = 128
 PACK = 4
@@ -33,6 +34,7 @@ def tile_tgcngraphconvolution_pa_kernel(tc, x, h, laplacian, weights, biases, ou
         keep = ctx.enter_context(tc.tile_pool(name="keep", bufs=1))
         first_banks = ctx.enter_context(tc.psum_pool(name="first_banks", bufs=4))
         second_banks = ctx.enter_context(tc.psum_pool(name="second_banks", bufs=4))
+        turn_about = ctx.enter_context(tc.tile_pool(name="turn_about", bufs=1))
         ctx.enter_context(tc.manual_schedule())
 
         ones = keep.tile([P, P], BF16)
@@ -77,13 +79,19 @@ def tile_tgcngraphconvolution_pa_kernel(tc, x, h, laplacian, weights, biases, ou
         ax_scales = []
         out_sb = []
         for b in range(B):
-            xh_grouped.append(keep.tile([P, 2, CH, HALF, PACK], BF16, name="xh_grouped%d" % b, align_bytes=64))
+            xh_grouped.append([keep.tile([P, CH, HALF, PACK], BF16, name="xh_grouped%d_%d" % (b, LOWER), align_bytes=64)])
+            if b < LATE:
+                xh_grouped[b].append(keep.tile([P, CH, HALF, PACK], BF16, name="xh_grouped%d_%d" % (b, UPPER), align_bytes=64))
             xh_codes.append(keep.tile([P, FEAT], U32, name="xh_codes%d" % b, align_bytes=64))
             xh_scales.append(keep.tile([P, FEAT], U8, name="xh_scales%d" % b, align_bytes=64))
-            ax_grouped.append(keep.tile([P, NODE_TILES, P, PACK], BF16, name="ax_grouped%d" % b, align_bytes=64))
+            ax_grouped.append([keep.tile([P, 2, P, PACK], BF16, name="ax_grouped%d_%d" % (b, half), align_bytes=64)
+                               for half in range(2)])
             ax_codes.append(keep.tile([P, NODES], U32, name="ax_codes%d" % b, align_bytes=64))
             ax_scales.append(keep.tile([P, NODES], U8, name="ax_scales%d" % b, align_bytes=64))
             out_sb.append(keep.tile([P, NODE_TILES, OUTS], F32, name="out_sb%d" % b))
+        xh_grouped[LATE].append(turn_about.tile([P, CH, HALF, PACK], BF16, tag="turn0", name="xh_grouped_turn", align_bytes=64))
+        ax_grouped[1][0] = turn_about.tile([P, 2, P, PACK], BF16, tag="turn1", name="ax_grouped_turn", align_bytes=64)
+        xh_beside = []
         plain_sb = [keep.tile([P, OUTS], F32, name="plain_sb%d" % j) for j in range(2)]
         out_rows = out.rearrange("b (p i d) o -> b p i (d o)", i=NODE_TILES, d=OUTS // 2)
         products = {}
@@ -92,19 +100,30 @@ def tile_tgcngraphconvolution_pa_kernel(tc, x, h, laplacian, weights, biases, ou
             return h_sb[b][:].rearrange("q (t g c) -> q g t c", t=PACK, c=CH)
 
         def regroup_lower(b):
-            nc.scalar.copy(out=xh_grouped[b][:, LOWER, :, 1:HALF, :].rearrange("q c g t -> q g t c"),
+            nc.scalar.copy(out=xh_grouped[b][LOWER][:, :, 1:HALF, :].rearrange("q c g t -> q g t c"),
                            in_=h_by_unit(b)[:, 1:GS - 2:2])
-            nc.scalar.copy(out=xh_grouped[b][:, LOWER, :, 0, :].rearrange("q c t -> q t c"),
+            nc.scalar.copy(out=xh_grouped[b][LOWER][:, :, 0, :].rearrange("q c t -> q t c"),
                            in_=x_sb[:, b].rearrange("q (t c) -> q t c", c=CH))
 
         def regroup_upper(b):
-            nc.vector.tensor_copy(out=xh_grouped[b][:, UPPER].rearrange("q c g t -> q g t c"),
+            nc.vector.tensor_copy(out=xh_grouped[b][UPPER][:].rearrange("q c g t -> q g t c"),
                                   in_=h_by_unit(b)[:, 0:GS - 1:2])
+
+        def regroup_upper_beside(c):
+            xh_beside.append(turn_about.tile([P, HALF, PACK], BF16, tag="turn%d" % c, name="xh_beside%d" % c, align_bytes=64))
+            nc.gpsimd.tensor_scalar(out=xh_beside[c][:], in0=h_by_unit(B - 1)[:, 0:GS - 1:2, :, c],
+                                    scalar1=1.0, scalar2=0.0, op0=MULT, op1=ADD)
+
+        def quantise_xh_beside():
+            for c in range(CH):
+                cols = slice((UPPER * CH + c) * HALF, (UPPER * CH + c + 1) * HALF)
+                nc.vector.quantize_mx(out=xh_codes[B - 1][:, cols].bitcast(FP8X4), scales=xh_scales[B - 1][:, cols],
+                                      in_=xh_beside[c][:].rearrange("q g t -> q (g t)"))
 
         def quantise_xh(b, half):
             cols = slice(half * CH * HALF, (half + 1) * CH * HALF)
             nc.vector.quantize_mx(out=xh_codes[b][:, cols].bitcast(FP8X4), scales=xh_scales[b][:, cols],
-                                  in_=xh_grouped[b][:, half].rearrange("q c g t -> q (c g t)"))
+                                  in_=xh_grouped[b][half][:].rearrange("q c g t -> q (c g t)"))
 
         lap_words = [lap_sb[pair][:].bitcast(F32) for pair in range(2)]
         lap_grouped_words = lap_grouped[:].bitcast(F32).rearrange("q (m u) -> q m u", u=2)
@@ -150,13 +169,13 @@ def tile_tgcngraphconvolution_pa_kernel(tc, x, h, laplacian, weights, biases, ou
                         rhs=lap_codes[:, i * P:(i + 1) * P].bitcast(FP8X4),
                         rhs_scale=lap_scales[:, i * P:(i + 1) * P],
                         start=True, stop=True)
-                nc.scalar.copy(out=ax_grouped[b][:, i], in_=bank[:].rearrange("p j m -> p m j"))
+                nc.scalar.copy(out=ax_grouped[b][i // 2][:, i % 2], in_=bank[:].rearrange("p j m -> p m j"))
 
         def quantise_ax(b, node_tiles):
             cols = slice(node_tiles[0] * P, (node_tiles[-1] + 1) * P)
             nc.vector.quantize_mx(
                 out=ax_codes[b][:, cols].bitcast(FP8X4), scales=ax_scales[b][:, cols],
-                in_=ax_grouped[b][:, node_tiles[0]:node_tiles[-1] + 1].rearrange("p i m j -> p (i m j)"))
+                in_=ax_grouped[b][node_tiles[0] // 2][:].rearrange("p i m j -> p (i m j)"))
 
         def second_matmul(b, node_tiles):
             for i in node_tiles:
@@ -219,7 +238,7 @@ def tile_tgcngraphconvolution_pa_kernel(tc, x, h, laplacian, weights, biases, ou
             if k <= last:
                 b, pair = groups[k]
                 ahead = b + 2
-                if ahead < B and pair[0] == 0:
+                if ahead == LATE and pair[0] == 0:
                     regroup_upper(ahead)
                 if k < last:
                     quantise_ax(b, pair)
@@ -228,10 +247,14 @@ def tile_tgcngraphconvolution_pa_kernel(tc, x, h, laplacian, weights, biases, ou
                 if k == 0:
                     quantise_weights()
                 second_matmul(b, pair)
-                if ahead < B and pair[0] != 0:
-                    quantise_xh(ahead, UPPER)
-                    if ahead != LATE:
-                        launch(ahead)
+                if (b, pair[0]) == (0, 2):
+                    quantise_xh(LATE, UPPER)
+                    regroup_upper_beside(0)
+                if (b, pair[0]) == (1, 0):
+                    regroup_upper_beside(1)
+                if (b, pair[0]) == (1, 2):
+                    quantise_xh_beside()
+                    launch(B - 1)
             if k - 1 == last - 2:
                 add_bias_beside(*groups[k - 1])
             elif k > 0:

@@ -21,9 +21,10 @@ FEAT = GS * CH
 OUTS = 512
 NODE_TILES = NODES // P
 HALF = GS // 2
-LOWER = 0
-UPPER = 1
-LATE = 2
+EVEN = 0
+ODD = 1
+FRONT = (0, 1)
+BACK = (2, 3)
 WARM_UP = 16
 FLOPS = 2 * 2 * B * NODES * FEAT * OUTS
 
@@ -32,35 +33,35 @@ def tile_tgcngraphconvolution_pa_kernel(tc, x, h, laplacian, weights, biases, ou
     nc = tc.nc
     with ExitStack() as ctx:
         keep = ctx.enter_context(tc.tile_pool(name="keep", bufs=1))
+        in_turn = ctx.enter_context(tc.tile_pool(name="in_turn", bufs=1))
         first_banks = ctx.enter_context(tc.psum_pool(name="first_banks", bufs=4))
         second_banks = ctx.enter_context(tc.psum_pool(name="second_banks", bufs=4))
-        turn_about = ctx.enter_context(tc.tile_pool(name="turn_about", bufs=1))
         ctx.enter_context(tc.manual_schedule())
 
-        ones = keep.tile([P, P], BF16)
-        nc.vector.memset(ones[:], 1.0)
         bias_row = keep.tile([P, OUTS], BF16)
         nc.vector.memset(bias_row[:], 0.0)
+        ones = keep.tile([P, P], BF16)
+        nc.vector.memset(ones[:], 1.0)
         identity = keep.tile([P, P], F32)
         make_identity(nc, identity[:])
 
-        lap_sb = [keep.tile([P, 2 * NODES], BF16, name="lap_sb%d" % pair) for pair in range(2)]
         x_sb = keep.tile([P, B, PACK * CH], BF16)
-        w_sb = keep.tile([P, 2, OUTS * CH], BF16)
         h_sb = [keep.tile([P, PACK * (FEAT - CH)], BF16, name="h_sb%d" % b) for b in range(B)]
+        lap_sb = [keep.tile([P, 2 * NODES], BF16, name="lap_sb%d" % pair) for pair in range(2)]
+        w_sb = keep.tile([P, 2, OUTS * CH], BF16)
         with nc.allow_non_contiguous_dma(reason="x has only two values a node"):
             nc.scalar.dma_start(out=x_sb[:], in_=x.rearrange("b (q t) c -> q b (t c)", t=PACK))
-        nc.scalar.dma_start(out=bias_row[0:1, :], in_=biases.rearrange("(a d) o -> a (d o)", a=1))
 
         def load_h(b):
             nc.sync.dma_start(out=h_sb[b][:], in_=h[b].rearrange("(q t) f -> q (t f)", t=PACK))
 
         load_h(0)
+        nc.sync.dma_start(out=bias_row[0:1, :], in_=biases.rearrange("(a d) o -> a (d o)", a=1))
         for pair in range(2):
-            nc.sync.dma_start(out=lap_sb[pair][:].rearrange("p (i n) -> p i n", i=2),
+            nc.sync.dma_start(out=lap_sb[pair][:].rearrange("p (j n) -> p j n", j=2),
                               in_=laplacian.rearrange("(p i) n -> p i n", i=NODE_TILES)[:, 2 * pair:2 * pair + 2, :])
         load_h(1)
-        nc.sync.dma_start(out=w_sb[:], in_=weights.rearrange("(p u) d c o -> p u (d c o)", u=2))
+        nc.sync.dma_start(out=w_sb[:], in_=weights.rearrange("(q u) d c o -> q u (d c o)", u=2))
         load_h(2)
         load_h(3)
 
@@ -71,72 +72,73 @@ def tile_tgcngraphconvolution_pa_kernel(tc, x, h, laplacian, weights, biases, ou
         w_grouped = keep.tile([P, OUTS, PACK], BF16, align_bytes=64)
         w_codes = keep.tile([P, OUTS], U32, align_bytes=64)
         w_scales = keep.tile([P, OUTS], U8, align_bytes=64)
-        xh_grouped = []
-        xh_codes = []
-        xh_scales = []
-        ax_grouped = []
-        ax_codes = []
-        ax_scales = []
-        out_sb = []
+        xh_grouped = {}
+        ax_grouped = {}
         for b in range(B):
-            xh_grouped.append([keep.tile([P, CH, HALF, PACK], BF16, name="xh_grouped%d_%d" % (b, LOWER), align_bytes=64)])
-            if b < LATE:
-                xh_grouped[b].append(keep.tile([P, CH, HALF, PACK], BF16, name="xh_grouped%d_%d" % (b, UPPER), align_bytes=64))
-            xh_codes.append(keep.tile([P, FEAT], U32, name="xh_codes%d" % b, align_bytes=64))
-            xh_scales.append(keep.tile([P, FEAT], U8, name="xh_scales%d" % b, align_bytes=64))
-            ax_grouped.append([keep.tile([P, 2, P, PACK], BF16, name="ax_grouped%d_%d" % (b, half), align_bytes=64)
-                               for half in range(2)])
-            ax_codes.append(keep.tile([P, NODES], U32, name="ax_codes%d" % b, align_bytes=64))
-            ax_scales.append(keep.tile([P, NODES], U8, name="ax_scales%d" % b, align_bytes=64))
-            out_sb.append(keep.tile([P, NODE_TILES, OUTS], F32, name="out_sb%d" % b))
-        xh_grouped[LATE].append(turn_about.tile([P, CH, HALF, PACK], BF16, tag="turn0", name="xh_grouped_turn", align_bytes=64))
-        ax_grouped[1][0] = turn_about.tile([P, 2, P, PACK], BF16, tag="turn1", name="ax_grouped_turn", align_bytes=64)
+            xh_grouped[(b, EVEN)] = keep.tile([P, CH, HALF, PACK], BF16, name="xh_even%d" % b, align_bytes=64)
+            ax_grouped[(b, BACK)] = keep.tile([P, 2, P, PACK], BF16, name="ax_back%d" % b, align_bytes=64)
+        for b in (0, 1):
+            xh_grouped[(b, ODD)] = keep.tile([P, CH, HALF, PACK], BF16, name="xh_odd%d" % b, align_bytes=64)
+        for b in (0, 2, 3):
+            ax_grouped[(b, FRONT)] = keep.tile([P, 2, P, PACK], BF16, name="ax_front%d" % b, align_bytes=64)
+        xh_grouped[(2, ODD)] = in_turn.tile([P, CH, HALF, PACK], BF16, tag="slot0", name="xh_odd2", align_bytes=64)
+        ax_grouped[(1, FRONT)] = in_turn.tile([P, 2, P, PACK], BF16, tag="slot1", name="ax_front1", align_bytes=64)
         xh_beside = []
-        plain_sb = [keep.tile([P, OUTS], F32, name="plain_sb%d" % j) for j in range(2)]
+        xh_codes = [keep.tile([P, FEAT], U32, name="xh_codes%d" % b, align_bytes=64) for b in range(B)]
+        xh_scales = [keep.tile([P, FEAT], U8, name="xh_scales%d" % b, align_bytes=64) for b in range(B)]
+        ax_codes = [keep.tile([P, NODES], U32, name="ax_codes%d" % b, align_bytes=64) for b in range(B)]
+        ax_scales = [keep.tile([P, NODES], U8, name="ax_scales%d" % b, align_bytes=64) for b in range(B)]
+        out_sb = [keep.tile([P, NODE_TILES, OUTS], F32, name="out_sb%d" % b) for b in range(B)]
+        no_bias_sb = [keep.tile([P, OUTS], F32, name="no_bias_sb%d" % j) for j in range(2)]
         out_rows = out.rearrange("b (p i d) o -> b p i (d o)", i=NODE_TILES, d=OUTS // 2)
         products = {}
 
-        def h_by_unit(b):
-            return h_sb[b][:].rearrange("q (t g c) -> q g t c", t=PACK, c=CH)
+        def warm_up():
+            bank = first_banks.tile([P, P], F32, tag="first", name="warm_bank")
+            for repeat in range(WARM_UP):
+                nc.tensor.matmul(out=bank[:], lhsT=ones[:], rhs=ones[:], start=True, stop=True)
 
-        def regroup_lower(b):
-            nc.scalar.copy(out=xh_grouped[b][LOWER][:, :, 1:HALF, :].rearrange("q c g t -> q g t c"),
+        def h_by_unit(b):
+            return h_sb[b][:].rearrange("q (t v c) -> q v t c", t=PACK, c=CH)
+
+        def regroup_even(b):
+            nc.scalar.copy(out=xh_grouped[(b, EVEN)][:, :, 1:HALF, :].rearrange("q c g t -> q g t c"),
                            in_=h_by_unit(b)[:, 1:GS - 2:2])
-            nc.scalar.copy(out=xh_grouped[b][LOWER][:, :, 0, :].rearrange("q c t -> q t c"),
+            nc.scalar.copy(out=xh_grouped[(b, EVEN)][:, :, 0, :].rearrange("q c t -> q t c"),
                            in_=x_sb[:, b].rearrange("q (t c) -> q t c", c=CH))
 
-        def regroup_upper(b):
-            nc.vector.tensor_copy(out=xh_grouped[b][UPPER][:].rearrange("q c g t -> q g t c"),
+        def regroup_odd(b):
+            nc.vector.tensor_copy(out=xh_grouped[(b, ODD)][:].rearrange("q c g t -> q g t c"),
                                   in_=h_by_unit(b)[:, 0:GS - 1:2])
 
-        def regroup_upper_beside(c):
-            xh_beside.append(turn_about.tile([P, HALF, PACK], BF16, tag="turn%d" % c, name="xh_beside%d" % c, align_bytes=64))
-            nc.gpsimd.tensor_scalar(out=xh_beside[c][:], in0=h_by_unit(B - 1)[:, 0:GS - 1:2, :, c],
+        def regroup_beside(c):
+            xh_beside.append(in_turn.tile([P, HALF, PACK], BF16, tag="slot%d" % c, name="xh_beside%d" % c, align_bytes=64))
+            nc.gpsimd.tensor_scalar(out=xh_beside[c][:], in0=h_by_unit(3)[:, 0:GS - 1:2, :, c],
                                     scalar1=1.0, scalar2=0.0, op0=MULT, op1=ADD)
-
-        def quantise_xh_beside():
-            for c in range(CH):
-                cols = slice((UPPER * CH + c) * HALF, (UPPER * CH + c + 1) * HALF)
-                nc.vector.quantize_mx(out=xh_codes[B - 1][:, cols].bitcast(FP8X4), scales=xh_scales[B - 1][:, cols],
-                                      in_=xh_beside[c][:].rearrange("q g t -> q (g t)"))
 
         def quantise_xh(b, half):
             cols = slice(half * CH * HALF, (half + 1) * CH * HALF)
             nc.vector.quantize_mx(out=xh_codes[b][:, cols].bitcast(FP8X4), scales=xh_scales[b][:, cols],
-                                  in_=xh_grouped[b][half][:].rearrange("q c g t -> q (c g t)"))
+                                  in_=xh_grouped[(b, half)][:].rearrange("q c g t -> q (c g t)"))
+
+        def quantise_xh_beside():
+            for c in range(CH):
+                cols = slice((ODD * CH + c) * HALF, (ODD * CH + c + 1) * HALF)
+                nc.vector.quantize_mx(out=xh_codes[3][:, cols].bitcast(FP8X4), scales=xh_scales[3][:, cols],
+                                      in_=xh_beside[c][:].rearrange("q g t -> q (g t)"))
 
         lap_words = [lap_sb[pair][:].bitcast(F32) for pair in range(2)]
-        lap_grouped_words = lap_grouped[:].bitcast(F32).rearrange("q (m u) -> q m u", u=2)
+        lap_grouped_words = lap_grouped[:].bitcast(F32).rearrange("q (col u) -> q col u", u=2)
 
         def transpose_laplacian(pair):
             bank = first_banks.tile([P, 2, 2, P], F32, tag="first", name="lap_t%d" % pair)
-            for i in range(2):
+            for j in range(2):
                 for u in range(2):
-                    start = i * 2 * P
-                    nc.tensor.transpose(bank[:, i, u, :], lap_words[pair][:, start + u:start + 2 * P:2], identity[:])
+                    start = j * 2 * P
+                    nc.tensor.transpose(bank[:, j, u, :], lap_words[pair][:, start + u:start + 2 * P:2], identity[:])
             nc.scalar.copy(
-                out=lap_grouped_words[:, 2 * P * pair:2 * P * (pair + 1), :].rearrange("q (i m) u -> q i m u", i=2),
-                in_=bank[:].rearrange("q i u m -> q i m u"))
+                out=lap_grouped_words[:, 2 * P * pair:2 * P * (pair + 1), :].rearrange("q (j p) u -> q j p u", j=2),
+                in_=bank[:].rearrange("q j u p -> q j p u"))
 
         def quantise_laplacian(pair):
             cols = slice(2 * P * pair, 2 * P * (pair + 1))
@@ -146,12 +148,12 @@ def tile_tgcngraphconvolution_pa_kernel(tc, x, h, laplacian, weights, biases, ou
         def regroup_weights(part):
             nc.vector.tensor_copy(
                 out=w_grouped[:, part * OUTS // 2:(part + 1) * OUTS // 2, :].rearrange(
-                    "p (d o) (u c) -> p d u c o", o=2, c=CH),
-                in_=w_sb[:, :, part * OUTS:(part + 1) * OUTS].rearrange("p u (d c o) -> p d u c o", c=CH, o=2))
+                    "q (d o) (u c) -> q d u c o", o=2, c=CH),
+                in_=w_sb[:, :, part * OUTS:(part + 1) * OUTS].rearrange("q u (d c o) -> q d u c o", c=CH, o=2))
 
         def quantise_weights():
             nc.vector.quantize_mx(out=w_codes[:].bitcast(FP8X4), scales=w_scales[:],
-                                  in_=w_grouped[:].rearrange("p n t -> p (n t)"))
+                                  in_=w_grouped[:].rearrange("q col t -> q (col t)"))
 
         def spread_bias():
             bank = second_banks.tile([P, OUTS], F32, tag="second", name="bias_bank")
@@ -161,24 +163,25 @@ def tile_tgcngraphconvolution_pa_kernel(tc, x, h, laplacian, weights, biases, ou
         def first_matmul(b):
             for i in range(NODE_TILES):
                 bank = first_banks.tile([P, PACK, P], F32, tag="first", name="ax_bank%d_%d" % (b, i))
-                for j in range(PACK):
+                for t in range(PACK):
                     nc.tensor.matmul_mx(
-                        out=bank[:, j, :],
-                        lhsT=xh_codes[b][:, j * P:(j + 1) * P].bitcast(FP8X4),
-                        lhsT_scale=xh_scales[b][:, j * P:(j + 1) * P],
+                        out=bank[:, t, :],
+                        lhsT=xh_codes[b][:, t * P:(t + 1) * P].bitcast(FP8X4),
+                        lhsT_scale=xh_scales[b][:, t * P:(t + 1) * P],
                         rhs=lap_codes[:, i * P:(i + 1) * P].bitcast(FP8X4),
                         rhs_scale=lap_scales[:, i * P:(i + 1) * P],
                         start=True, stop=True)
-                nc.scalar.copy(out=ax_grouped[b][i // 2][:, i % 2], in_=bank[:].rearrange("p j m -> p m j"))
+                group = FRONT if i in FRONT else BACK
+                nc.scalar.copy(out=ax_grouped[(b, group)][:, group.index(i)], in_=bank[:].rearrange("q t p -> q p t"))
 
-        def quantise_ax(b, node_tiles):
-            cols = slice(node_tiles[0] * P, (node_tiles[-1] + 1) * P)
+        def quantise_ax(b, group):
+            cols = slice(group[0] * P, (group[-1] + 1) * P)
             nc.vector.quantize_mx(
                 out=ax_codes[b][:, cols].bitcast(FP8X4), scales=ax_scales[b][:, cols],
-                in_=ax_grouped[b][node_tiles[0] // 2][:].rearrange("p i m j -> p (i m j)"))
+                in_=ax_grouped[(b, group)][:].rearrange("q j p t -> q (j p t)"))
 
-        def second_matmul(b, node_tiles):
-            for i in node_tiles:
+        def second_matmul(b, group):
+            for i in group:
                 bank = second_banks.tile([P, OUTS], F32, tag="second", name="out_bank%d_%d" % (b, i))
                 products[(b, i)] = bank
                 nc.tensor.matmul_mx(
@@ -189,81 +192,81 @@ def tile_tgcngraphconvolution_pa_kernel(tc, x, h, laplacian, weights, biases, ou
                     rhs_scale=w_scales[:],
                     start=True, stop=True)
 
-        def add_bias(b, i):
-            nc.vector.tensor_tensor(out=out_sb[b][:, i, :], in0=products[(b, i)][:], in1=bias_sb[:], op=ADD)
+        def finish(b, group, tile_by_tile=False):
+            for i in group:
+                nc.vector.tensor_tensor(out=out_sb[b][:, i, :], in0=products[(b, i)][:], in1=bias_sb[:], op=ADD)
+                if tile_by_tile:
+                    nc.sync.dma_start(out=out_rows[b][:, i:i + 1, :], in_=out_sb[b][:, i:i + 1, :])
+            if not tile_by_tile:
+                nc.sync.dma_start(out=out_rows[b][:, group[0]:group[-1] + 1, :],
+                                  in_=out_sb[b][:, group[0]:group[-1] + 1, :])
 
-        def add_bias_beside(b, node_tiles):
-            for i in node_tiles:
-                nc.scalar.copy(out=plain_sb[i % 2][:], in_=products[(b, i)][:])
-            for i in node_tiles:
-                nc.gpsimd.tensor_tensor(out=out_sb[b][:, i, :], in0=plain_sb[i % 2][:], in1=bias_sb[:], op=ADD)
-            for i in node_tiles:
+        def finish_beside(b, group):
+            for i in group:
+                nc.scalar.copy(out=no_bias_sb[i % 2][:], in_=products[(b, i)][:])
+            for i in group:
+                nc.gpsimd.tensor_tensor(out=out_sb[b][:, i, :], in0=no_bias_sb[i % 2][:], in1=bias_sb[:], op=ADD)
+            for i in group:
                 nc.scalar.dma_start(out=out_rows[b][:, i:i + 1, :], in_=out_sb[b][:, i:i + 1, :])
 
-        def store(b, node_tiles):
-            nc.sync.dma_start(out=out_rows[b][:, node_tiles[0]:node_tiles[-1] + 1, :],
-                              in_=out_sb[b][:, node_tiles[0]:node_tiles[-1] + 1, :])
-
-        def launch(b):
-            quantise_xh(b, LOWER)
-            if b + 1 < B:
-                regroup_lower(b + 1)
-            first_matmul(b)
-
-        warm_bank = first_banks.tile([P, P], F32, tag="first", name="warm_bank")
-        for w in range(WARM_UP):
-            nc.tensor.matmul(out=warm_bank[:], lhsT=ones[:], rhs=ones[:], start=True, stop=True)
-        regroup_upper(0)
-        regroup_lower(0)
-        quantise_xh(0, UPPER)
-        quantise_xh(0, LOWER)
+        warm_up()
+        regroup_odd(0)
+        regroup_even(0)
+        quantise_xh(0, ODD)
+        quantise_xh(0, EVEN)
+        spread_bias()
         transpose_laplacian(0)
         transpose_laplacian(1)
         quantise_laplacian(0)
-        regroup_upper(1)
+        regroup_odd(1)
         quantise_laplacian(1)
-        regroup_lower(1)
-        quantise_xh(1, UPPER)
+        regroup_even(1)
+        quantise_xh(1, ODD)
         regroup_weights(0)
-        quantise_xh(1, LOWER)
+        quantise_xh(1, EVEN)
         regroup_weights(1)
         first_matmul(0)
-        spread_bias()
-        regroup_lower(LATE)
+        regroup_even(2)
         first_matmul(1)
 
-        groups = [(b, pair) for b in range(B) for pair in ((0, 1), (2, 3))]
-        last = len(groups) - 1
-        for k in range(last + 2):
-            if k <= last:
-                b, pair = groups[k]
-                ahead = b + 2
-                if ahead == LATE and pair[0] == 0:
-                    regroup_upper(ahead)
-                if k < last:
-                    quantise_ax(b, pair)
-                if k == last - 1:
-                    quantise_ax(*groups[last])
-                if k == 0:
-                    quantise_weights()
-                second_matmul(b, pair)
-                if (b, pair[0]) == (0, 2):
-                    quantise_xh(LATE, UPPER)
-                    regroup_upper_beside(0)
-                if (b, pair[0]) == (1, 0):
-                    regroup_upper_beside(1)
-                if (b, pair[0]) == (1, 2):
-                    quantise_xh_beside()
-                    launch(B - 1)
-            if k - 1 == last - 2:
-                add_bias_beside(*groups[k - 1])
-            elif k > 0:
-                b, pair = groups[k - 1]
-                for i in pair:
-                    add_bias(b, i)
-                    if k - 1 >= last - 1:
-                        store(b, (i,))
-                if k - 1 < last - 1:
-                    store(b, pair)
-                if k - 1 == 0:
-                    launch(LATE)
+        regroup_odd(2)
+        quantise_ax(0, FRONT)
+        quantise_weights()
+        second_matmul(0, FRONT)
+
+        quantise_ax(0, BACK)
+        second_matmul(0, BACK)
+        quantise_xh(2, ODD)
+        regroup_beside(0)
+        finish(0, FRONT)
+        quantise_xh(2, EVEN)
+        regroup_even(3)
+        first_matmul(2)
+
+        quantise_ax(1, FRONT)
+        second_matmul(1, FRONT)
+        regroup_beside(1)
+        finish(0, BACK)
+
+        quantise_ax(1, BACK)
+        second_matmul(1, BACK)
+        quantise_xh_beside()
+        quantise_xh(3, EVEN)
+        first_matmul(3)
+        finish(1, FRONT)
+
+        quantise_ax(2, FRONT)
+        second_matmul(2, FRONT)
+        finish(1, BACK)
+
+        quantise_ax(2, BACK)
+        second_matmul(2, BACK)
+        finish(2, FRONT)
+
+        quantise_ax(3, FRONT)
+        quantise_ax(3, BACK)
+        second_matmul(3, FRONT)
+        finish_beside(2, BACK)
+        second_matmul(3, BACK)
+        finish(3, FRONT, tile_by_tile=True)
+        finish(3, BACK, tile_by_tile=True)

@@ -261,11 +261,11 @@ def tile_tgcngraphconvolution_pa_kernel(tc, x, h, laplacian, weights, biases, ou
 
         quantise_ax(2, BACK)
         second_matmul(2, BACK)
+        quantise_ax(3, FRONT)
         finish(2, FRONT)
 
-        quantise_ax(3, FRONT)
-        quantise_ax(3, BACK)
         second_matmul(3, FRONT)
+        quantise_ax(3, BACK)
         finish_beside(2, BACK)
         second_matmul(3, BACK)
         finish(3, FRONT, tile_by_tile=True)

@@ -229,10 +229,10 @@ def tile_tgcngraphconvolution_pa_kernel(tc, x, h, laplacian, weights, biases, ou
         regroup_even(2)
         first_matmul(1)
 
-        regroup_odd(2)
         quantise_ax(0, FRONT)
         quantise_weights()
         second_matmul(0, FRONT)
+        regroup_odd(2)
 
         quantise_ax(0, BACK)
         second_matmul(0, BACK)

@@ -38,8 +38,6 @@ def tile_tgcngraphconvolution_pa_kernel(tc, x, h, laplacian, weights, biases, ou
         second_banks = ctx.enter_context(tc.psum_pool(name="second_banks", bufs=4))
         ctx.enter_context(tc.manual_schedule())
 
-        bias_row = keep.tile([P, OUTS], BF16)
-        nc.vector.memset(bias_row[:], 0.0)
         ones = keep.tile([P, P], BF16)
         nc.vector.memset(ones[:], 1.0)
         identity = keep.tile([P, P], F32)
@@ -49,23 +47,25 @@ def tile_tgcngraphconvolution_pa_kernel(tc, x, h, laplacian, weights, biases, ou
         h_sb = [keep.tile([P, PACK * (FEAT - CH)], BF16, name="h_sb%d" % b) for b in range(B)]
         lap_sb = [keep.tile([P, 2 * NODES], BF16, name="lap_sb%d" % pair) for pair in range(2)]
         w_sb = keep.tile([P, 2, OUTS * CH], BF16)
-        with nc.allow_non_contiguous_dma(reason="x has only two values a node"):
-            nc.scalar.dma_start(out=x_sb[:], in_=x.rearrange("b (q t) c -> q b (t c)", t=PACK))
-
+        bias_sb = keep.tile([P, OUTS], BF16)
         def load_h(b):
             nc.sync.dma_start(out=h_sb[b][:], in_=h[b].rearrange("(q t) f -> q (t f)", t=PACK))
 
         load_h(0)
-        nc.sync.dma_start(out=bias_row[0:1, :], in_=biases.rearrange("(a d) o -> a (d o)", a=1))
-        for pair in range(2):
+        def load_laplacian(pair):
             nc.sync.dma_start(out=lap_sb[pair][:].rearrange("p (j n) -> p j n", j=2),
                               in_=laplacian.rearrange("(p i) n -> p i n", i=NODE_TILES)[:, 2 * pair:2 * pair + 2, :])
+
+        load_laplacian(0)
+        load_laplacian(1)
+        with nc.allow_non_contiguous_dma(reason="x has only two values a node"):
+            nc.sync.dma_start(out=x_sb[:], in_=x.rearrange("b (q t) c -> q b (t c)", t=PACK))
         load_h(1)
         nc.sync.dma_start(out=w_sb[:], in_=weights.rearrange("(q u) d c o -> q u (d c o)", u=2))
         load_h(2)
+        nc.sync.dma_start(out=bias_sb[:], in_=biases.rearrange("d o -> (d o)").partition_broadcast(P))
         load_h(3)
 
-        bias_sb = keep.tile([P, OUTS], F32)
         lap_grouped = keep.tile([P, NODES * PACK], BF16, align_bytes=64)
         lap_codes = keep.tile([P, NODES], U32, align_bytes=64)
         lap_scales = keep.tile([P, NODES], U8, align_bytes=64)
@@ -136,7 +136,8 @@ def tile_tgcngraphconvolution_pa_kernel(tc, x, h, laplacian, weights, biases, ou
                 for u in range(2):
                     start = j * 2 * P
                     nc.tensor.transpose(bank[:, j, u, :], lap_words[pair][:, start + u:start + 2 * P:2], identity[:])
-            nc.scalar.copy(
+            copy = nc.vector.tensor_copy if pair == 0 else nc.scalar.copy
+            copy(
                 out=lap_grouped_words[:, 2 * P * pair:2 * P * (pair + 1), :].rearrange("q (j p) u -> q j p u", j=2),
                 in_=bank[:].rearrange("q j u p -> q j p u"))
 
@@ -154,11 +155,6 @@ def tile_tgcngraphconvolution_pa_kernel(tc, x, h, laplacian, weights, biases, ou
         def quantise_weights():
             nc.vector.quantize_mx(out=w_codes[:].bitcast(FP8X4), scales=w_scales[:],
                                   in_=w_grouped[:].rearrange("q col t -> q (col t)"))
-
-        def spread_bias():
-            bank = second_banks.tile([P, OUTS], F32, tag="second", name="bias_bank")
-            nc.tensor.matmul(out=bank[:], lhsT=ones[:], rhs=bias_row[:], start=True, stop=True)
-            nc.scalar.copy(out=bias_sb[:], in_=bank[:])
 
         def first_matmul(b):
             for i in range(NODE_TILES):
@@ -213,9 +209,8 @@ def tile_tgcngraphconvolution_pa_kernel(tc, x, h, laplacian, weights, biases, ou
         regroup_odd(0)
         regroup_even(0)
         quantise_xh(0, ODD)
-        quantise_xh(0, EVEN)
-        spread_bias()
         transpose_laplacian(0)
+        quantise_xh(0, EVEN)
         transpose_laplacian(1)
         quantise_laplacian(0)
         regroup_odd(1)

@@ -38,6 +38,8 @@ def tile_tgcngraphconvolution_pa_kernel(tc, x, h, laplacian, weights, biases, ou
         second_banks = ctx.enter_context(tc.psum_pool(name="second_banks", bufs=4))
         ctx.enter_context(tc.manual_schedule())
 
+        bias_row = keep.tile([P, OUTS], BF16)
+        nc.vector.memset(bias_row[:], 0.0)
         ones = keep.tile([P, P], BF16)
         nc.vector.memset(ones[:], 1.0)
         identity = keep.tile([P, P], F32)
@@ -56,6 +58,7 @@ def tile_tgcngraphconvolution_pa_kernel(tc, x, h, laplacian, weights, biases, ou
             nc.sync.dma_start(out=lap_sb[pair][:].rearrange("p (j n) -> p j n", j=2),
                               in_=laplacian.rearrange("(p i) n -> p i n", i=NODE_TILES)[:, 2 * pair:2 * pair + 2, :])
 
+        nc.sync.dma_start(out=bias_row[0:1, :], in_=biases.rearrange("(a d) o -> a (d o)", a=1))
         load_laplacian(0)
         load_laplacian(1)
         with nc.allow_non_contiguous_dma(reason="x has only two values a node"):
@@ -63,7 +66,6 @@ def tile_tgcngraphconvolution_pa_kernel(tc, x, h, laplacian, weights, biases, ou
         load_h(1)
         nc.sync.dma_start(out=w_sb[:], in_=weights.rearrange("(q u) d c o -> q u (d c o)", u=2))
         load_h(2)
-        nc.sync.dma_start(out=bias_sb[:], in_=biases.rearrange("d o -> (d o)").partition_broadcast(P))
         load_h(3)
 
         lap_grouped = keep.tile([P, NODES * PACK], BF16, align_bytes=64)
@@ -156,6 +158,11 @@ def tile_tgcngraphconvolution_pa_kernel(tc, x, h, laplacian, weights, biases, ou
             nc.vector.quantize_mx(out=w_codes[:].bitcast(FP8X4), scales=w_scales[:],
                                   in_=w_grouped[:].rearrange("q col t -> q (col t)"))
 
+        def spread_bias():
+            bank = second_banks.tile([P, OUTS], BF16, tag="second", name="bias_bank")
+            nc.tensor.matmul(out=bank[:], lhsT=ones[:], rhs=bias_row[:], start=True, stop=True)
+            nc.scalar.copy(out=bias_sb[:].bitcast(F32), in_=bank[:].bitcast(F32))
+
         def first_matmul(b):
             for i in range(NODE_TILES):
                 bank = first_banks.tile([P, PACK, P], F32, tag="first", name="ax_bank%d_%d" % (b, i))
@@ -209,6 +216,7 @@ def tile_tgcngraphconvolution_pa_kernel(tc, x, h, laplacian, weights, biases, ou
         regroup_odd(0)
         regroup_even(0)
         quantise_xh(0, ODD)
+        spread_bias()
         transpose_laplacian(0)
         quantise_xh(0, EVEN)
         transpose_laplacian(1)

@@ -78,11 +78,13 @@ def tile_tgcngraphconvolution_pa_kernel(tc, x, h, laplacian, weights, biases, ou
         ax_grouped = {}
         for b in range(B):
             xh_grouped[(b, EVEN)] = keep.tile([P, CH, HALF, PACK], BF16, name="xh_even%d" % b, align_bytes=64)
-            ax_grouped[(b, BACK)] = keep.tile([P, 2, P, PACK], BF16, name="ax_back%d" % b, align_bytes=64)
+            if b < 3:
+                ax_grouped[(b, BACK)] = keep.tile([P, 2, P, PACK], BF16, name="ax_back%d" % b, align_bytes=64)
         for b in (0, 1):
             xh_grouped[(b, ODD)] = keep.tile([P, CH, HALF, PACK], BF16, name="xh_odd%d" % b, align_bytes=64)
         for b in (0, 2, 3):
             ax_grouped[(b, FRONT)] = keep.tile([P, 2, P, PACK], BF16, name="ax_front%d" % b, align_bytes=64)
+        ax_grouped[(3, BACK)] = in_turn.tile([P, 2, P, PACK], BF16, tag="slot2", name="ax_back3", align_bytes=64)
         xh_grouped[(2, ODD)] = in_turn.tile([P, CH, HALF, PACK], BF16, tag="slot0", name="xh_odd2", align_bytes=64)
         ax_grouped[(1, FRONT)] = in_turn.tile([P, 2, P, PACK], BF16, tag="slot1", name="ax_front1", align_bytes=64)
         xh_beside = []
@@ -163,8 +165,8 @@ def tile_tgcngraphconvolution_pa_kernel(tc, x, h, laplacian, weights, biases, ou
             nc.tensor.matmul(out=bank[:], lhsT=ones[:], rhs=bias_row[:], start=True, stop=True)
             nc.scalar.copy(out=bias_sb[:].bitcast(F32), in_=bank[:].bitcast(F32))
 
-        def first_matmul(b):
-            for i in range(NODE_TILES):
+        def first_matmul(b, tiles=range(NODE_TILES)):
+            for i in tiles:
                 bank = first_banks.tile([P, PACK, P], F32, tag="first", name="ax_bank%d_%d" % (b, i))
                 for t in range(PACK):
                     nc.tensor.matmul_mx(
@@ -195,22 +197,17 @@ def tile_tgcngraphconvolution_pa_kernel(tc, x, h, laplacian, weights, biases, ou
                     rhs_scale=w_scales[:],
                     start=True, stop=True)
 
-        def finish(b, group, tile_by_tile=False):
+        def store(b, i, source, queue):
+            queue.dma_start(out=out_rows[b][:, i:i + 1, :], in_=source)
+
+        def finish(b, group):
             for i in group:
                 nc.vector.tensor_tensor(out=out_sb[b][:, i, :], in0=products[(b, i)][:], in1=bias_sb[:], op=ADD)
-                if tile_by_tile:
-                    nc.sync.dma_start(out=out_rows[b][:, i:i + 1, :], in_=out_sb[b][:, i:i + 1, :])
-            if not tile_by_tile:
-                nc.sync.dma_start(out=out_rows[b][:, group[0]:group[-1] + 1, :],
-                                  in_=out_sb[b][:, group[0]:group[-1] + 1, :])
+                store(b, i, out_sb[b][:, i:i + 1, :], nc.sync)
 
-        def finish_beside(b, group):
-            for i in group:
-                nc.scalar.copy(out=no_bias_sb[i % 2][:], in_=products[(b, i)][:])
-            for i in group:
-                nc.gpsimd.tensor_tensor(out=out_sb[b][:, i, :], in0=no_bias_sb[i % 2][:], in1=bias_sb[:], op=ADD)
-            for i in group:
-                nc.scalar.dma_start(out=out_rows[b][:, i:i + 1, :], in_=out_sb[b][:, i:i + 1, :])
+        def finish_beside(b, i, total):
+            nc.scalar.copy(out=no_bias_sb[b % 2][:], in_=products[(b, i)][:])
+            nc.gpsimd.tensor_tensor(out=total, in0=no_bias_sb[b % 2][:], in1=bias_sb[:], op=ADD)
 
         warm_up()
         regroup_odd(0)
@@ -255,21 +252,27 @@ def tile_tgcngraphconvolution_pa_kernel(tc, x, h, laplacian, weights, biases, ou
         second_matmul(1, BACK)
         quantise_xh_beside()
         quantise_xh(3, EVEN)
-        first_matmul(3)
+        first_matmul(3, FRONT)
+        finish_beside(1, 3, out_sb[1][:, 3, :])
+        first_matmul(3, BACK)
         finish(1, FRONT)
 
         quantise_ax(2, FRONT)
         second_matmul(2, FRONT)
-        finish(1, BACK)
+        finish(1, (2,))
 
         quantise_ax(2, BACK)
         second_matmul(2, BACK)
         quantise_ax(3, FRONT)
         finish(2, FRONT)
-
         second_matmul(3, FRONT)
+        store(1, 3, out_sb[1][:, 3:4, :], nc.sync)
+        finish(2, (2,))
+
         quantise_ax(3, BACK)
-        finish_beside(2, BACK)
+        late_sb = in_turn.tile([P, 1, OUTS], F32, tag="slot2", name="late_sb", align_bytes=64)
+        finish_beside(2, 3, late_sb[:, 0, :])
+        store(2, 3, late_sb[:], nc.scalar)
         second_matmul(3, BACK)
-        finish(3, FRONT, tile_by_tile=True)
-        finish(3, BACK, tile_by_tile=True)
+        finish(3, FRONT)
+        finish(3, BACK)

@@ -25,7 +25,7 @@ EVEN = 0
 ODD = 1
 FRONT = (0, 1)
 BACK = (2, 3)
-WARM_UP = 16
+WARM_UP = 18
 FLOPS = 2 * 2 * B * NODES * FEAT * OUTS
 
 
@@ -165,9 +165,11 @@ def tile_tgcngraphconvolution_pa_kernel(tc, x, h, laplacian, weights, biases, ou
             nc.tensor.matmul(out=bank[:], lhsT=ones[:], rhs=bias_row[:], start=True, stop=True)
             nc.scalar.copy(out=bias_sb[:].bitcast(F32), in_=bank[:].bitcast(F32))
 
-        def first_matmul(b, tiles=range(NODE_TILES)):
+        def first_matmul(b, tiles=range(NODE_TILES), idle=0):
             for i in tiles:
                 bank = first_banks.tile([P, PACK, P], F32, tag="first", name="ax_bank%d_%d" % (b, i))
+                for repeat in range(idle if i == 0 else 0):
+                    nc.tensor.matmul(out=bank[:, 0, :], lhsT=ones[:], rhs=ones[:], start=True, stop=True)
                 for t in range(PACK):
                     nc.tensor.matmul_mx(
                         out=bank[:, t, :],
@@ -225,9 +227,9 @@ def tile_tgcngraphconvolution_pa_kernel(tc, x, h, laplacian, weights, biases, ou
         regroup_weights(0)
         quantise_xh(1, EVEN)
         regroup_weights(1)
-        first_matmul(0)
+        first_matmul(0, idle=6)
         regroup_even(2)
-        first_matmul(1)
+        first_matmul(1, idle=4)
 
         quantise_ax(0, FRONT)
         quantise_weights()
@@ -241,7 +243,7 @@ def tile_tgcngraphconvolution_pa_kernel(tc, x, h, laplacian, weights, biases, ou
         finish(0, FRONT)
         quantise_xh(2, EVEN)
         regroup_even(3)
-        first_matmul(2)
+        first_matmul(2, idle=8)
 
         quantise_ax(1, FRONT)
         second_matmul(1, FRONT)

@@ -74,18 +74,21 @@ def tile_tgcngraphconvolution_pa_kernel(tc, x, h, laplacian, weights, biases, ou
         w_grouped = keep.tile([P, OUTS, PACK], BF16, align_bytes=64)
         w_codes = keep.tile([P, OUTS], U32, align_bytes=64)
         w_scales = keep.tile([P, OUTS], U8, align_bytes=64)
+        xh_even = keep.tile([P, B, CH, HALF, PACK], BF16, align_bytes=64)
         xh_grouped = {}
         ax_grouped = {}
         for b in range(B):
-            xh_grouped[(b, EVEN)] = keep.tile([P, CH, HALF, PACK], BF16, name="xh_even%d" % b, align_bytes=64)
+            xh_grouped[(b, EVEN)] = xh_even[:, b]
             if b < 3:
                 ax_grouped[(b, BACK)] = keep.tile([P, 2, P, PACK], BF16, name="ax_back%d" % b, align_bytes=64)
         for b in (0, 1):
-            xh_grouped[(b, ODD)] = keep.tile([P, CH, HALF, PACK], BF16, name="xh_odd%d" % b, align_bytes=64)
+            xh_odd = keep.tile([P, CH, HALF, PACK], BF16, name="xh_odd%d" % b, align_bytes=64)
+            xh_grouped[(b, ODD)] = xh_odd[:]
         for b in (0, 2, 3):
             ax_grouped[(b, FRONT)] = keep.tile([P, 2, P, PACK], BF16, name="ax_front%d" % b, align_bytes=64)
         ax_grouped[(3, BACK)] = in_turn.tile([P, 2, P, PACK], BF16, tag="slot2", name="ax_back3", align_bytes=64)
-        xh_grouped[(2, ODD)] = in_turn.tile([P, CH, HALF, PACK], BF16, tag="slot0", name="xh_odd2", align_bytes=64)
+        xh_odd2 = in_turn.tile([P, CH, HALF, PACK], BF16, tag="slot0", name="xh_odd2", align_bytes=64)
+        xh_grouped[(2, ODD)] = xh_odd2[:]
         ax_grouped[(1, FRONT)] = in_turn.tile([P, 2, P, PACK], BF16, tag="slot1", name="ax_front1", align_bytes=64)
         xh_beside = []
         xh_codes = [keep.tile([P, FEAT], U32, name="xh_codes%d" % b, align_bytes=64) for b in range(B)]
@@ -108,11 +111,13 @@ def tile_tgcngraphconvolution_pa_kernel(tc, x, h, laplacian, weights, biases, ou
         def regroup_even(b):
             nc.scalar.copy(out=xh_grouped[(b, EVEN)][:, :, 1:HALF, :].rearrange("q c g t -> q g t c"),
                            in_=h_by_unit(b)[:, 1:GS - 2:2])
-            nc.scalar.copy(out=xh_grouped[(b, EVEN)][:, :, 0, :].rearrange("q c t -> q t c"),
-                           in_=x_sb[:, b].rearrange("q (t c) -> q t c", c=CH))
+
+        def regroup_x():
+            nc.scalar.copy(out=xh_even[:, :, :, 0, :].rearrange("q b c t -> q b t c"),
+                           in_=x_sb[:].rearrange("q b (t c) -> q b t c", c=CH))
 
         def regroup_odd(b):
-            nc.vector.tensor_copy(out=xh_grouped[(b, ODD)][:].rearrange("q c g t -> q g t c"),
+            nc.vector.tensor_copy(out=xh_grouped[(b, ODD)].rearrange("q c g t -> q g t c"),
                                   in_=h_by_unit(b)[:, 0:GS - 1:2])
 
         def regroup_beside(c):
@@ -123,7 +128,7 @@ def tile_tgcngraphconvolution_pa_kernel(tc, x, h, laplacian, weights, biases, ou
         def quantise_xh(b, half):
             cols = slice(half * CH * HALF, (half + 1) * CH * HALF)
             nc.vector.quantize_mx(out=xh_codes[b][:, cols].bitcast(FP8X4), scales=xh_scales[b][:, cols],
-                                  in_=xh_grouped[(b, half)][:].rearrange("q c g t -> q (c g t)"))
+                                  in_=xh_grouped[(b, half)].rearrange("q c g t -> q (c g t)"))
 
         def quantise_xh_beside():
             for c in range(CH):
@@ -187,9 +192,11 @@ def tile_tgcngraphconvolution_pa_kernel(tc, x, h, laplacian, weights, biases, ou
                 out=ax_codes[b][:, cols].bitcast(FP8X4), scales=ax_scales[b][:, cols],
                 in_=ax_grouped[(b, group)][:].rearrange("q j p t -> q (j p t)"))
 
-        def second_matmul(b, group):
+        def second_matmul(b, group, idle=0):
             for i in group:
                 bank = second_banks.tile([P, OUTS], F32, tag="second", name="out_bank%d_%d" % (b, i))
+                for repeat in range(idle if i == group[0] else 0):
+                    nc.tensor.matmul(out=bank[:, 0:P], lhsT=ones[:], rhs=ones[:], start=True, stop=True)
                 products[(b, i)] = bank
                 nc.tensor.matmul_mx(
                     out=bank[:],
@@ -214,6 +221,7 @@ def tile_tgcngraphconvolution_pa_kernel(tc, x, h, laplacian, weights, biases, ou
         warm_up()
         regroup_odd(0)
         regroup_even(0)
+        regroup_x()
         quantise_xh(0, ODD)
         spread_bias()
         transpose_laplacian(0)
@@ -265,8 +273,9 @@ def tile_tgcngraphconvolution_pa_kernel(tc, x, h, laplacian, weights, biases, ou
 
         quantise_ax(2, BACK)
         second_matmul(2, BACK)
+        finish(2, (0,))
         quantise_ax(3, FRONT)
-        finish(2, FRONT)
+        finish(2, (1,))
         second_matmul(3, FRONT)
         store(1, 3, out_sb[1][:, 3:4, :], nc.sync)
         finish(2, (2,))
@@ -275,6 +284,6 @@ def tile_tgcngraphconvolution_pa_kernel(tc, x, h, laplacian, weights, biases, ou
         late_sb = in_turn.tile([P, 1, OUTS], F32, tag="slot2", name="late_sb", align_bytes=64)
         finish_beside(2, 3, late_sb[:, 0, :])
         store(2, 3, late_sb[:], nc.scalar)
-        second_matmul(3, BACK)
+        second_matmul(3, BACK, idle=4)
         finish(3, FRONT)
         finish(3, BACK)

@@ -96,7 +96,7 @@ def tile_tgcngraphconvolution_pa_kernel(tc, x, h, laplacian, weights, biases, ou
         ax_codes = [keep.tile([P, NODES], U32, name="ax_codes%d" % b, align_bytes=64) for b in range(B)]
         ax_scales = [keep.tile([P, NODES], U8, name="ax_scales%d" % b, align_bytes=64) for b in range(B)]
         out_sb = [keep.tile([P, NODE_TILES, OUTS], F32, name="out_sb%d" % b) for b in range(B)]
-        no_bias_sb = [keep.tile([P, OUTS], F32, name="no_bias_sb%d" % j) for j in range(2)]
+        no_bias_sb = [keep.tile([P, OUTS], F32, name="no_bias_sb%d" % j) for j in range(3)]
         out_rows = out.rearrange("b (p i d) o -> b p i (d o)", i=NODE_TILES, d=OUTS // 2)
         products = {}
 
@@ -214,9 +214,9 @@ def tile_tgcngraphconvolution_pa_kernel(tc, x, h, laplacian, weights, biases, ou
                 nc.vector.tensor_tensor(out=out_sb[b][:, i, :], in0=products[(b, i)][:], in1=bias_sb[:], op=ADD)
                 store(b, i, out_sb[b][:, i:i + 1, :], nc.sync)
 
-        def finish_beside(b, i, total):
-            nc.scalar.copy(out=no_bias_sb[b % 2][:], in_=products[(b, i)][:])
-            nc.gpsimd.tensor_tensor(out=total, in0=no_bias_sb[b % 2][:], in1=bias_sb[:], op=ADD)
+        def finish_beside(b, i, no_bias, total):
+            nc.scalar.copy(out=no_bias[:], in_=products[(b, i)][:])
+            nc.gpsimd.tensor_tensor(out=total, in0=no_bias[:], in1=bias_sb[:], op=ADD)
 
         warm_up()
         regroup_odd(0)
@@ -263,7 +263,7 @@ def tile_tgcngraphconvolution_pa_kernel(tc, x, h, laplacian, weights, biases, ou
         quantise_xh_beside()
         quantise_xh(3, EVEN)
         first_matmul(3, FRONT)
-        finish_beside(1, 3, out_sb[1][:, 3, :])
+        finish_beside(1, 3, no_bias_sb[0], out_sb[1][:, 3, :])
         first_matmul(3, BACK)
         finish(1, FRONT)
 
@@ -278,12 +278,13 @@ def tile_tgcngraphconvolution_pa_kernel(tc, x, h, laplacian, weights, biases, ou
         finish(2, (1,))
         second_matmul(3, FRONT)
         store(1, 3, out_sb[1][:, 3:4, :], nc.sync)
-        finish(2, (2,))
 
         quantise_ax(3, BACK)
         late_sb = in_turn.tile([P, 1, OUTS], F32, tag="slot2", name="late_sb", align_bytes=64)
-        finish_beside(2, 3, late_sb[:, 0, :])
-        store(2, 3, late_sb[:], nc.scalar)
+        finish_beside(2, 2, no_bias_sb[1], late_sb[:, 0, :])
+        finish_beside(2, 3, no_bias_sb[2], out_sb[2][:, 3, :])
+        store(2, 2, late_sb[:], nc.scalar)
+        store(2, 3, out_sb[2][:, 3:4, :], nc.scalar)
         second_matmul(3, BACK, idle=4)
         finish(3, FRONT)
         finish(3, BACK)

from contextlib import ExitStack

import concourse.mybir as mybir
from concourse.masks import make_identity

F32 = mybir.dt.float32
BF16 = mybir.dt.bfloat16
U32 = mybir.dt.uint32
U8 = mybir.dt.uint8
FP8X4 = mybir.dt.float8_e4m3fn_x4
ADD = mybir.AluOpType.add
MULT = mybir.AluOpType.mult

P = 128
PACK = 4
B = 4
NODES = 512
CH = 2
GS = 256
FEAT = GS * CH
OUTS = 512
NODE_TILES = NODES // P
HALF = GS // 2
EVEN = 0
ODD = 1
FRONT = (0, 1)
BACK = (2, 3)
WARM_UP = 18
FLOPS = 2 * 2 * B * NODES * FEAT * OUTS


def tile_tgcngraphconvolution_pa_kernel(tc, x, h, laplacian, weights, biases, out):
    nc = tc.nc
    with ExitStack() as ctx:
        keep = ctx.enter_context(tc.tile_pool(name="keep", bufs=1))
        in_turn = ctx.enter_context(tc.tile_pool(name="in_turn", bufs=1))
        first_banks = ctx.enter_context(tc.psum_pool(name="first_banks", bufs=4))
        second_banks = ctx.enter_context(tc.psum_pool(name="second_banks", bufs=4))
        ctx.enter_context(tc.manual_schedule())

        bias_row = keep.tile([P, OUTS], BF16)
        nc.vector.memset(bias_row[:], 0.0)
        ones = keep.tile([P, P], BF16)
        nc.vector.memset(ones[:], 1.0)
        identity = keep.tile([P, P], F32)
        make_identity(nc, identity[:])

        x_sb = keep.tile([P, B, PACK * CH], BF16)
        h_sb = [keep.tile([P, PACK * (FEAT - CH)], BF16, name="h_sb%d" % b) for b in range(B)]
        lap_sb = [keep.tile([P, 2 * NODES], BF16, name="lap_sb%d" % pair) for pair in range(2)]
        w_sb = keep.tile([P, 2, OUTS * CH], BF16)
        bias_sb = keep.tile([P, OUTS], BF16)
        def load_h(b):
            nc.sync.dma_start(out=h_sb[b][:], in_=h[b].rearrange("(q t) f -> q (t f)", t=PACK))

        load_h(0)
        def load_laplacian(pair):
            nc.sync.dma_start(out=lap_sb[pair][:].rearrange("p (j n) -> p j n", j=2),
                              in_=laplacian.rearrange("(p i) n -> p i n", i=NODE_TILES)[:, 2 * pair:2 * pair + 2, :])

        nc.sync.dma_start(out=bias_row[0:1, :], in_=biases.rearrange("(a d) o -> a (d o)", a=1))
        load_laplacian(0)
        load_laplacian(1)
        with nc.allow_non_contiguous_dma(reason="x has only two values a node"):
            nc.sync.dma_start(out=x_sb[:], in_=x.rearrange("b (q t) c -> q b (t c)", t=PACK))
        load_h(1)
        nc.sync.dma_start(out=w_sb[:], in_=weights.rearrange("(q u) d c o -> q u (d c o)", u=2))
        load_h(2)
        load_h(3)

        lap_grouped = keep.tile([P, NODES * PACK], BF16, align_bytes=64)
        lap_codes = keep.tile([P, NODES], U32, align_bytes=64)
        lap_scales = keep.tile([P, NODES], U8, align_bytes=64)
        w_grouped = keep.tile([P, OUTS, PACK], BF16, align_bytes=64)
        w_codes = keep.tile([P, OUTS], U32, align_bytes=64)
        w_scales = keep.tile([P, OUTS], U8, align_bytes=64)
        xh_even = keep.tile([P, B, CH, HALF, PACK], BF16, align_bytes=64)
        xh_grouped = {}
        ax_grouped = {}
        for b in range(B):
            xh_grouped[(b, EVEN)] = xh_even[:, b]
            if b < 3:
                ax_grouped[(b, BACK)] = keep.tile([P, 2, P, PACK], BF16, name="ax_back%d" % b, align_bytes=64)
        for b in (0, 1):
            xh_odd = keep.tile([P, CH, HALF, PACK], BF16, name="xh_odd%d" % b, align_bytes=64)
            xh_grouped[(b, ODD)] = xh_odd[:]
        for b in (0, 2, 3):
            ax_grouped[(b, FRONT)] = keep.tile([P, 2, P, PACK], BF16, name="ax_front%d" % b, align_bytes=64)
        ax_grouped[(3, BACK)] = in_turn.tile([P, 2, P, PACK], BF16, tag="slot2", name="ax_back3", align_bytes=64)
        xh_odd2 = in_turn.tile([P, CH, HALF, PACK], BF16, tag="slot0", name="xh_odd2", align_bytes=64)
        xh_grouped[(2, ODD)] = xh_odd2[:]
        ax_grouped[(1, FRONT)] = in_turn.tile([P, 2, P, PACK], BF16, tag="slot1", name="ax_front1", align_bytes=64)
        xh_beside = []
        xh_codes = [keep.tile([P, FEAT], U32, name="xh_codes%d" % b, align_bytes=64) for b in range(B)]
        xh_scales = [keep.tile([P, FEAT], U8, name="xh_scales%d" % b, align_bytes=64) for b in range(B)]
        ax_codes = [keep.tile([P, NODES], U32, name="ax_codes%d" % b, align_bytes=64) for b in range(B)]
        ax_scales = [keep.tile([P, NODES], U8, name="ax_scales%d" % b, align_bytes=64) for b in range(B)]
        out_sb = [keep.tile([P, NODE_TILES, OUTS], F32, name="out_sb%d" % b) for b in range(B)]
        no_bias_sb = [keep.tile([P, OUTS], F32, name="no_bias_sb%d" % j) for j in range(3)]
        out_rows = out.rearrange("b (p i d) o -> b p i (d o)", i=NODE_TILES, d=OUTS // 2)
        products = {}

        def warm_up():
            bank = first_banks.tile([P, P], F32, tag="first", name="warm_bank")
            for repeat in range(WARM_UP):
                nc.tensor.matmul(out=bank[:], lhsT=ones[:], rhs=ones[:], start=True, stop=True)

        def h_by_unit(b):
            return h_sb[b][:].rearrange("q (t v c) -> q v t c", t=PACK, c=CH)

        def regroup_even(b):
            nc.scalar.copy(out=xh_grouped[(b, EVEN)][:, :, 1:HALF, :].rearrange("q c g t -> q g t c"),
                           in_=h_by_unit(b)[:, 1:GS - 2:2])

        def regroup_x():
            nc.scalar.copy(out=xh_even[:, :, :, 0, :].rearrange("q b c t -> q b t c"),
                           in_=x_sb[:].rearrange("q b (t c) -> q b t c", c=CH))

        def regroup_odd(b):
            nc.vector.tensor_copy(out=xh_grouped[(b, ODD)].rearrange("q c g t -> q g t c"),
                                  in_=h_by_unit(b)[:, 0:GS - 1:2])

        def regroup_beside(c):
            xh_beside.append(in_turn.tile([P, HALF, PACK], BF16, tag="slot%d" % c, name="xh_beside%d" % c, align_bytes=64))
            nc.gpsimd.tensor_scalar(out=xh_beside[c][:], in0=h_by_unit(3)[:, 0:GS - 1:2, :, c],
                                    scalar1=1.0, scalar2=0.0, op0=MULT, op1=ADD)

        def quantise_xh(b, half):
            cols = slice(half * CH * HALF, (half + 1) * CH * HALF)
            nc.vector.quantize_mx(out=xh_codes[b][:, cols].bitcast(FP8X4), scales=xh_scales[b][:, cols],
                                  in_=xh_grouped[(b, half)].rearrange("q c g t -> q (c g t)"))

        def quantise_xh_beside():
            for c in range(CH):
                cols = slice((ODD * CH + c) * HALF, (ODD * CH + c + 1) * HALF)
                nc.vector.quantize_mx(out=xh_codes[3][:, cols].bitcast(FP8X4), scales=xh_scales[3][:, cols],
                                      in_=xh_beside[c][:].rearrange("q g t -> q (g t)"))

        lap_words = [lap_sb[pair][:].bitcast(F32) for pair in range(2)]
        lap_grouped_words = lap_grouped[:].bitcast(F32).rearrange("q (col u) -> q col u", u=2)

        def transpose_laplacian(pair):
            bank = first_banks.tile([P, 2, 2, P], F32, tag="first", name="lap_t%d" % pair)
            for j in range(2):
                for u in range(2):
                    start = j * 2 * P
                    nc.tensor.transpose(bank[:, j, u, :], lap_words[pair][:, start + u:start + 2 * P:2], identity[:])
            copy = nc.vector.tensor_copy if pair == 0 else nc.scalar.copy
            copy(
                out=lap_grouped_words[:, 2 * P * pair:2 * P * (pair + 1), :].rearrange("q (j p) u -> q j p u", j=2),
                in_=bank[:].rearrange("q j u p -> q j p u"))

        def quantise_laplacian(pair):
            cols = slice(2 * P * pair, 2 * P * (pair + 1))
            nc.vector.quantize_mx(out=lap_codes[:, cols].bitcast(FP8X4), scales=lap_scales[:, cols],
                                  in_=lap_grouped[:, 2 * P * PACK * pair:2 * P * PACK * (pair + 1)])

        def regroup_weights(part):
            nc.vector.tensor_copy(
                out=w_grouped[:, part * OUTS // 2:(part + 1) * OUTS // 2, :].rearrange(
                    "q (d o) (u c) -> q d u c o", o=2, c=CH),
                in_=w_sb[:, :, part * OUTS:(part + 1) * OUTS].rearrange("q u (d c o) -> q d u c o", c=CH, o=2))

        def quantise_weights():
            nc.vector.quantize_mx(out=w_codes[:].bitcast(FP8X4), scales=w_scales[:],
                                  in_=w_grouped[:].rearrange("q col t -> q (col t)"))

        def spread_bias():
            bank = second_banks.tile([P, OUTS], BF16, tag="second", name="bias_bank")
            nc.tensor.matmul(out=bank[:], lhsT=ones[:], rhs=bias_row[:], start=True, stop=True)
            nc.scalar.copy(out=bias_sb[:].bitcast(F32), in_=bank[:].bitcast(F32))

        def first_matmul(b, tiles=range(NODE_TILES), idle=0):
            for i in tiles:
                bank = first_banks.tile([P, PACK, P], F32, tag="first", name="ax_bank%d_%d" % (b, i))
                for repeat in range(idle if i == 0 else 0):
                    nc.tensor.matmul(out=bank[:, 0, :], lhsT=ones[:], rhs=ones[:], start=True, stop=True)
                for t in range(PACK):
                    nc.tensor.matmul_mx(
                        out=bank[:, t, :],
                        lhsT=xh_codes[b][:, t * P:(t + 1) * P].bitcast(FP8X4),
                        lhsT_scale=xh_scales[b][:, t * P:(t + 1) * P],
                        rhs=lap_codes[:, i * P:(i + 1) * P].bitcast(FP8X4),
                        rhs_scale=lap_scales[:, i * P:(i + 1) * P],
                        start=True, stop=True)
                group = FRONT if i in FRONT else BACK
                nc.scalar.copy(out=ax_grouped[(b, group)][:, group.index(i)], in_=bank[:].rearrange("q t p -> q p t"))

        def quantise_ax(b, group):
            cols = slice(group[0] * P, (group[-1] + 1) * P)
            nc.vector.quantize_mx(
                out=ax_codes[b][:, cols].bitcast(FP8X4), scales=ax_scales[b][:, cols],
                in_=ax_grouped[(b, group)][:].rearrange("q j p t -> q (j p t)"))

        def second_matmul(b, group, idle=0):
            for i in group:
                bank = second_banks.tile([P, OUTS], F32, tag="second", name="out_bank%d_%d" % (b, i))
                for repeat in range(idle if i == group[0] else 0):
                    nc.tensor.matmul(out=bank[:, 0:P], lhsT=ones[:], rhs=ones[:], start=True, stop=True)
                products[(b, i)] = bank
                nc.tensor.matmul_mx(
                    out=bank[:],
                    lhsT=ax_codes[b][:, i * P:(i + 1) * P].bitcast(FP8X4),
                    lhsT_scale=ax_scales[b][:, i * P:(i + 1) * P],
                    rhs=w_codes[:].bitcast(FP8X4),
                    rhs_scale=w_scales[:],
                    start=True, stop=True)

        def store(b, i, source, queue):
            queue.dma_start(out=out_rows[b][:, i:i + 1, :], in_=source)

        def finish(b, group):
            for i in group:
                nc.vector.tensor_tensor(out=out_sb[b][:, i, :], in0=products[(b, i)][:], in1=bias_sb[:], op=ADD)
                store(b, i, out_sb[b][:, i:i + 1, :], nc.sync)

        def finish_beside(b, i, no_bias, total):
            nc.scalar.copy(out=no_bias[:], in_=products[(b, i)][:])
            nc.gpsimd.tensor_tensor(out=total, in0=no_bias[:], in1=bias_sb[:], op=ADD)

        warm_up()
        regroup_odd(0)
        regroup_even(0)
        regroup_x()
        quantise_xh(0, ODD)
        spread_bias()
        transpose_laplacian(0)
        quantise_xh(0, EVEN)
        transpose_laplacian(1)
        quantise_laplacian(0)
        regroup_odd(1)
        quantise_laplacian(1)
        regroup_even(1)
        quantise_xh(1, ODD)
        regroup_weights(0)
        quantise_xh(1, EVEN)
        regroup_weights(1)
        first_matmul(0, idle=6)
        regroup_even(2)
        first_matmul(1, idle=4)

        quantise_ax(0, FRONT)
        quantise_weights()
        second_matmul(0, FRONT)
        regroup_odd(2)

        quantise_ax(0, BACK)
        second_matmul(0, BACK)
        quantise_xh(2, ODD)
        regroup_beside(0)
        finish(0, FRONT)
        quantise_xh(2, EVEN)
        regroup_even(3)
        first_matmul(2, idle=8)

        quantise_ax(1, FRONT)
        second_matmul(1, FRONT)
        regroup_beside(1)
        finish(0, BACK)

        quantise_ax(1, BACK)
        second_matmul(1, BACK)
        quantise_xh_beside()
        quantise_xh(3, EVEN)
        first_matmul(3, FRONT)
        finish_beside(1, 3, no_bias_sb[0], out_sb[1][:, 3, :])
        first_matmul(3, BACK)
        finish(1, FRONT)

        quantise_ax(2, FRONT)
        second_matmul(2, FRONT)
        finish(1, (2,))

        quantise_ax(2, BACK)
        second_matmul(2, BACK)
        finish(2, (0,))
        quantise_ax(3, FRONT)
        finish(2, (1,))
        second_matmul(3, FRONT)
        store(1, 3, out_sb[1][:, 3:4, :], nc.sync)

        quantise_ax(3, BACK)
        late_sb = in_turn.tile([P, 1, OUTS], F32, tag="slot2", name="late_sb", align_bytes=64)
        finish_beside(2, 2, no_bias_sb[1], late_sb[:, 0, :])
        finish_beside(2, 3, no_bias_sb[2], out_sb[2][:, 3, :])
        store(2, 2, late_sb[:], nc.scalar)
        store(2, 3, out_sb[2][:, 3:4, :], nc.scalar)
        second_matmul(3, BACK, idle=4)
        finish(3, FRONT)
        finish(3, BACK)
